import numpy as np
import ml_dtypes


def mxq(x, axis, fmt="e4m3"):
    dtype, down = {"e4m3": (ml_dtypes.float8_e4m3fn, 7), "e5m2": (ml_dtypes.float8_e5m2, 14)}[fmt]
    v = np.moveaxis(np.asarray(x, np.float32).astype(ml_dtypes.bfloat16).astype(np.float64), axis, -1)
    blocks = v.reshape(v.shape[:-1] + (-1, 32))
    amax = np.abs(blocks).max(-1, keepdims=True)
    byte = np.maximum(np.where(amax > 0, np.frexp(amax)[1] - 1 + 127, 0) - down, 1)
    scale = np.exp2(byte - 127.0)
    codes = (blocks / scale).astype(np.float32).astype(dtype).astype(np.float64)
    return np.moveaxis((codes * scale).reshape(v.shape), -1, axis)


WIDE = False


def mx_kscale(k):
    if not WIDE:
        return np.ones(k)
    levels = np.array([10, -10, 5, -5, 0])
    if k % 512:
        return np.exp2(np.random.permutation(np.resize(levels, k // 32))).repeat(32)
    a = np.empty((k // 512, 16))
    for p in range(k // 512):
        a[p, :8] = np.random.permutation(np.resize(levels, 8))
        for g in range(8):
            far = levels[np.abs(levels - a[p, g]) >= 10]
            a[p, g + 8] = far[np.random.randint(len(far))]
    return np.exp2(a.ravel()).repeat(32)


BF16 = ml_dtypes.bfloat16


def bf(x):
    return np.asarray(x, np.float32).astype(BF16)


def f64(x):
    return np.asarray(x).astype(np.float64)


B, S, D, F1, F2, F3, F4 = 128, 4, 256, 1024, 2048, 1024, 512
K = D + D


def setup_inputs():
    s, t = mx_kscale(K), mx_kscale(F1)
    return {"x1": bf(np.random.standard_normal((B, S, D)) * s[:D]),
            "x2": bf(np.random.standard_normal((B, S, D)) * s[D:]),
            "W1": bf(np.random.standard_normal((S, K, F1)) * 1.0 / np.sqrt(K) / s[None, :, None] * t[None, None, :]),
            "b1": bf(np.random.standard_normal((S, F1)) * 0.3 * t),
            "W2": bf(np.random.standard_normal((S, F1, F2)) * 1.4 / np.sqrt(F1) / t[None, :, None]),
            "b2": bf(np.random.standard_normal((S, F2)) * 0.3)}


def reference(x1, x2, W1, b1, W2, b2):
    x = np.concatenate([f64(x1), f64(x2)], axis=-1).transpose(1, 0, 2)
    h = np.maximum(f64(bf(mxq(x, 2, "e4m3") @ mxq(f64(W1), 1, "e4m3"))) + f64(b1)[:, None, :], 0.0)
    y = (mxq(h, 2, "e4m3") @ mxq(f64(W2), 1, "e4m3")) + f64(b2)[:, None, :]
    return y.transpose(1, 0, 2)

@@ -1,0 +1,293 @@
+from contextlib import ExitStack
+
+import concourse.mybir as mybir
+from concourse.masks import make_identity
+
+B, S, D, F1, F2 = 128, 4, 256, 1024, 2048
+K1 = 2 * D
+FLOPS = 2 * B * S * (K1 * F1 + F1 * F2)
+
+F32 = mybir.dt.float32
+BF16 = mybir.dt.bfloat16
+U32 = mybir.dt.uint32
+U8 = mybir.dt.uint8
+FP8X4 = mybir.dt.float8_e4m3fn_x4
+RELU = mybir.ActivationFunctionType.Relu
+ADD = mybir.AluOpType.add
+MAX = mybir.AluOpType.max
+
+P = 128
+PACK = 4
+BANK_DT = BF16
+S_SHARE_32 = [15, 21]
+S_SHARE_32_LAST = [19, 23]
+MS = 56
+FAST = True
+MANUAL = True
+W2_BUFS = 5
+EVAC_ON_VECTOR = False
+SUB = 1024
+PIECES = [[1024, 1024], [1024, 1024], [1024, 1024], [1024, 512, 256, 256]]
+
+
+def interleave(copy, dst, src):
+    if FAST:
+        copy(
+            out=dst.rearrange("p (c i j) -> p c j i", i=4, j=PACK),
+            in_=src.rearrange("p j (c i) -> p c j i", i=4),
+        )
+    else:
+        copy(
+            out=dst.rearrange("p (w j) -> p w j", j=PACK),
+            in_=src.rearrange("p j w -> p w j"),
+        )
+
+
+def tile_simplefusionmodule_pa_kernel(tc, x1, x2, W1, b1, W2, b2, out):
+    nc = tc.nc
+    with ExitStack() as ctx:
+        const = ctx.enter_context(tc.tile_pool(name="const", bufs=1))
+        w1raw_pool = ctx.enter_context(tc.tile_pool(name="w1raw", bufs=S))
+        w2raw_pool = ctx.enter_context(tc.tile_pool(name="w2raw", bufs=W2_BUFS))
+        grp_pool = ctx.enter_context(tc.tile_pool(name="grp", bufs=4))
+        code_pool = ctx.enter_context(tc.tile_pool(name="code", bufs=3))
+        h_pool = ctx.enter_context(tc.tile_pool(name="hpool", bufs=2))
+        o_pool = ctx.enter_context(tc.tile_pool(name="opool", bufs=4))
+        psum = ctx.enter_context(tc.psum_pool(name="psum", bufs=8))
+        if MANUAL:
+            ctx.enter_context(tc.manual_schedule())
+
+        warm_in = const.tile([P, 1], F32, name="warm_in")
+        warm_out = const.tile([P, 1], F32, name="warm_out")
+        nc.vector.memset(warm_in[:], 0.0)
+        nc.scalar.activation(out=warm_out[:], in_=warm_in[:], func=RELU)
+        ident = const.tile([P, P], F32, name="ident")
+        make_identity(nc, ident[:])
+
+        w1raw = []
+        for s in range(S):
+            w1raw_t = w1raw_pool.tile([P, PACK, F1], BF16, name="w1raw_t", tag="w1raw")
+            w1raw.append(w1raw_t)
+        w1view = [W1[s].rearrange("(p j) c -> p j c", j=PACK) for s in range(S)]
+        x_sb = const.tile([P, S, K1], BF16, name="x_sb")
+        b1col = const.tile([P, 2 * S, PACK], BF16, name="b1col")
+        b2t = const.tile([P, S * F2], BF16, name="b2t")
+
+        nc.sync.dma_start(out=w1raw[0][:, :, 0:512], in_=w1view[0][:, :, 0:512])
+        nc.sync.dma_start(out=x_sb[:, :, 0:D], in_=x1)
+        nc.sync.dma_start(out=x_sb[:, :, D:K1], in_=x2)
+        nc.sync.dma_start(out=w1raw[0][:, :, 512:1024], in_=w1view[0][:, :, 512:1024])
+        for s in range(1, S):
+            nc.sync.dma_start(out=w1raw[s][:], in_=w1view[s])
+            if s == 1:
+                nc.sync.dma_start(out=b1col[:], in_=b1.rearrange("s (g p t) -> p (s g) t", g=2, t=PACK))
+
+        chunks = [(s, g) for s in range(S) for g in range(2)]
+        w2raw = {}
+
+        def load_chunk(q):
+            s, g = chunks[q]
+            if g == 1:
+                nc.sync.dma_start(out=b2t[:, s * F2 : (s + 1) * F2], in_=b2[s].partition_broadcast(P))
+            raw = w2raw_pool.tile([P, PACK, F2], BF16, name="w2raw_t", tag="w2raw")
+            view = W2[s, 512 * g : 512 * (g + 1), :].rearrange("(p j) n -> p j n", j=PACK)
+            if q == len(chunks) - 1:
+                c0 = 0
+                for w in PIECES[s]:
+                    nc.sync.dma_start(out=raw[:, :, c0 : c0 + w], in_=view[:, :, c0 : c0 + w])
+                    c0 += w
+            else:
+                nc.sync.dma_start(out=raw[:], in_=view)
+            w2raw[q] = raw
+
+        for q in range(W2_BUFS):
+            load_chunk(q)
+
+        x_words = x_sb[:].rearrange("p s k -> p (s k)").bitcast(F32)
+        x_grouped = const.tile([P, S * P * PACK], BF16, name="x_grouped", align_bytes=64)
+        x_codes = const.tile([P, S * P], U32, name="x_codes", align_bytes=64)
+        x_scales = const.tile([P, S * P], U8, name="x_scales", align_bytes=64)
+
+        def x_prepare():
+            for half in range(2):
+                xt = psum.tile([P, 2, 2, P], F32, name="xt", tag="bank")
+                for s2 in range(2):
+                    s = 2 * half + s2
+                    for u in range(2):
+                        nc.tensor.transpose(
+                            xt[:, s2, u, :], x_words[:, 256 * s + u : 256 * (s + 1) : 2], ident[:]
+                        )
+                nc.scalar.copy(
+                    out=x_grouped[:, half * 1024 : (half + 1) * 1024]
+                    .bitcast(F32)
+                    .rearrange("p (s b u) -> p s b u", s=2, u=2),
+                    in_=xt[:].rearrange("p s u b -> p s b u"),
+                )
+
+        def x_quant():
+            nc.vector.quantize_mx(out=x_codes[:].bitcast(FP8X4), scales=x_scales[:], in_=x_grouped[:])
+
+        h_codes = []
+        h_scales = []
+        for s in range(S):
+            h_codes_t = const.tile([P, 2 * P], U32, name="h_codes%d" % s, align_bytes=64)
+            h_scales_t = const.tile([P, 2 * P], U8, name="h_scales%d" % s, align_bytes=64)
+            h_codes.append(h_codes_t)
+            h_scales.append(h_scales_t)
+
+        st = {}
+        items = []
+        for s in range(S):
+            for g in range(2):
+                c0 = 0
+                for w in PIECES[s]:
+                    items.append((s, c0, w, g))
+                    c0 += w
+        NA = S
+
+        def width_of(i):
+            if i < NA:
+                return SUB
+            return items[i - NA][2]
+
+        def quant(i):
+            w = width_of(i)
+            codes = code_pool.tile([P, SUB], U32, name="codes", tag="codes", align_bytes=64)
+            scales = code_pool.tile([P, SUB], U8, name="scales", tag="scales", align_bytes=64)
+            nc.vector.quantize_mx(
+                out=codes[:, 0:w].bitcast(FP8X4), scales=scales[:, 0:w], in_=st[("g", i)][:, 0 : PACK * w]
+            )
+            st[("c", i)] = (codes, scales)
+
+        def a_copy(i):
+            s = i
+            grouped = grp_pool.tile([P, PACK * SUB], BF16, name="grouped", tag="grouped", align_bytes=64)
+            for G in range(2):
+                if i == 0 and G == 1:
+                    x_prepare()
+                dst = grouped[:, G * 2048 : (G + 1) * 2048].rearrange("p (t m j) -> p t m j", t=4, j=PACK)
+                src = w1raw[s][:, :, G * 512 : (G + 1) * 512].rearrange("p j (m t) -> p t m j", t=4)
+                nc.scalar.copy(out=dst[:, :, 0:MS, :], in_=src[:, :, 0:MS, :])
+                nc.vector.tensor_copy(out=dst[:, :, MS:P, :], in_=src[:, :, MS:P, :])
+            st[("g", i)] = grouped
+
+        def a_mm(i):
+            s = i
+            codes, scales = st[("c", i)]
+            banks = []
+            for G in range(2):
+                hp = psum.tile([P, 4, P], BANK_DT, name="hp", tag="bank")
+                for t in range(4):
+                    cols = slice(G * 512 + t * P, G * 512 + (t + 1) * P)
+                    nc.tensor.matmul_mx(
+                        out=hp[:, t, :],
+                        lhsT=codes[:, cols].bitcast(FP8X4),
+                        lhsT_scale=scales[:, cols],
+                        rhs=x_codes[:, s * P : (s + 1) * P].bitcast(FP8X4),
+                        rhs_scale=x_scales[:, s * P : (s + 1) * P],
+                        start=True,
+                        stop=True,
+                    )
+                banks.append(hp)
+            st[("hp", i)] = banks
+
+        def a_evac(i):
+            s = i
+            hT = h_pool.tile([P, 2, 4, P], BF16, name="hT", tag="hT")
+            for G in range(2):
+                hp = st[("hp", i)][G]
+                for t in range(4):
+                    bias = b1col[:, 2 * s + G, t : t + 1]
+                    if EVAC_ON_VECTOR:
+                        nc.vector.tensor_scalar(
+                            out=hT[:, G, t, :], in0=hp[:, t, :], scalar1=bias, scalar2=0.0, op0=ADD, op1=MAX
+                        )
+                    else:
+                        nc.scalar.activation(out=hT[:, G, t, :], in_=hp[:, t, :], func=RELU, bias=bias)
+            st[("hT", i)] = hT
+
+        def a_inter(i):
+            hg = h_pool.tile([P, 2 * P * PACK], BF16, name="hg", tag="hg", align_bytes=64)
+            nc.vector.tensor_copy(
+                out=hg[:].rearrange("p (g b t) -> p g b t", g=2, t=PACK),
+                in_=st[("hT", i)][:].rearrange("p g t b -> p g b t"),
+            )
+            st[("hg", i)] = hg
+
+        def a_hquant(i):
+            s = i
+            nc.vector.quantize_mx(out=h_codes[s][:].bitcast(FP8X4), scales=h_scales[s][:], in_=st[("hg", i)][:])
+
+        def b_copy(i):
+            s, c0, w, g = items[i - NA]
+            q = 2 * s + g
+            sc = w * (S_SHARE_32_LAST if s == S - 1 else S_SHARE_32)[g] // 32
+            grouped = grp_pool.tile([P, PACK * SUB], BF16, name="grouped", tag="grouped", align_bytes=64)
+            src = w2raw[q][:, :, c0 : c0 + w]
+            interleave(nc.scalar.copy, grouped[:, 0 : PACK * sc], src[:, :, 0:sc])
+            interleave(nc.vector.tensor_copy, grouped[:, PACK * sc : PACK * w], src[:, :, sc:w])
+            st[("g", i)] = grouped
+            if c0 + w == F2 and q + W2_BUFS < len(chunks):
+                load_chunk(q + W2_BUFS)
+
+        def b_mm(i):
+            s, c0, w, g = items[i - NA]
+            codes, scales = st[("c", i)]
+            nw = min(w, 512)
+            for nt in range(w // nw):
+                if g == 0:
+                    acc = psum.tile([P, 512], F32, name="acc", tag="bank")
+                    st[("acc", s, c0, nt)] = acc
+                acc = st[("acc", s, c0, nt)]
+                nc.tensor.matmul_mx(
+                    out=acc[:, 0:nw],
+                    lhsT=h_codes[s][:, g * P : (g + 1) * P].bitcast(FP8X4),
+                    lhsT_scale=h_scales[s][:, g * P : (g + 1) * P],
+                    rhs=codes[:, nt * nw : (nt + 1) * nw].bitcast(FP8X4),
+                    rhs_scale=scales[:, nt * nw : (nt + 1) * nw],
+                    start=(g == 0),
+                    stop=(g == 1),
+                )
+
+        def b_post(i):
+            s, c0, w, g = items[i - NA]
+            if g == 0:
+                return
+            nw = min(w, 512)
+            o_sb = o_pool.tile([P, SUB], F32, name="o_sb", tag="o_sb")
+            for nt in range(w // nw):
+                n0 = s * F2 + c0 + nt * nw
+                nc.vector.tensor_tensor(
+                    out=o_sb[:, nt * nw : (nt + 1) * nw],
+                    in0=st[("acc", s, c0, nt)][:, 0:nw],
+                    in1=b2t[:, n0 : n0 + nw],
+                    op=ADD,
+                )
+            nc.sync.dma_start(out=out[:, s, c0 : c0 + w], in_=o_sb[:, 0:w])
+
+        n = NA + len(items)
+        for i in range(n + 4):
+            if i < NA:
+                a_copy(i)
+            elif i < n:
+                b_copy(i)
+            if i == 1:
+                x_quant()
+            k = i - 1
+            if 0 <= k < n:
+                quant(k)
+                if k < NA:
+                    a_mm(k)
+                else:
+                    b_mm(k)
+            k = i - 2
+            if 0 <= k < NA:
+                a_evac(k)
+            elif NA <= k < n:
+                b_post(k)
+            k = i - 3
+            if 0 <= k < NA:
+                a_inter(k)
+            k = i - 4
+            if 0 <= k < NA:
+                a_hquant(k)

@@ -21,7 +21,7 @@ PACK = 4
 BANK_DT = BF16
 S_SHARE_32 = [15, 21]
 S_SHARE_32_LAST = [19, 23]
-MS = 56
+MS = 32
 FAST = True
 MANUAL = True
 W2_BUFS = 5
@@ -63,6 +63,11 @@ def tile_simplefusionmodule_pa_kernel(tc, x1, x2, W1, b1, W2, b2, out):
         nc.scalar.activation(out=warm_out[:], in_=warm_in[:], func=RELU)
         ident = const.tile([P, P], F32, name="ident")
         make_identity(nc, ident[:])
+        identb = const.tile([P, P], BF16, name="identb")
+        make_identity(nc, identb[:])
+        b2rows = const.tile([P, P], BF16, name="b2rows")
+        b2col = const.tile([P, 64], BF16, name="b2col")
+        nc.vector.memset(b2rows[64:128, :], 0.0)
 
         w1raw = []
         for s in range(S):
@@ -73,6 +78,7 @@ def tile_simplefusionmodule_pa_kernel(tc, x1, x2, W1, b1, W2, b2, out):
         b1col = const.tile([P, 2 * S, PACK], BF16, name="b1col")
         b2t = const.tile([P, S * F2], BF16, name="b2t")
 
+        nc.sync.dma_start(out=b2rows[0:64, :], in_=b2.rearrange("s (j c) -> (s j) c", c=P))
         nc.sync.dma_start(out=w1raw[0][:, :, 0:512], in_=w1view[0][:, :, 0:512])
         nc.sync.dma_start(out=x_sb[:, :, 0:D], in_=x1)
         nc.sync.dma_start(out=x_sb[:, :, D:K1], in_=x2)
@@ -87,8 +93,6 @@ def tile_simplefusionmodule_pa_kernel(tc, x1, x2, W1, b1, W2, b2, out):
 
         def load_chunk(q):
             s, g = chunks[q]
-            if g == 1:
-                nc.sync.dma_start(out=b2t[:, s * F2 : (s + 1) * F2], in_=b2[s].partition_broadcast(P))
             raw = w2raw_pool.tile([P, PACK, F2], BF16, name="w2raw_t", tag="w2raw")
             view = W2[s, 512 * g : 512 * (g + 1), :].rearrange("(p j) n -> p j n", j=PACK)
             if q == len(chunks) - 1:
@@ -127,6 +131,26 @@ def tile_simplefusionmodule_pa_kernel(tc, x1, x2, W1, b1, W2, b2, out):
         def x_quant():
             nc.vector.quantize_mx(out=x_codes[:].bitcast(FP8X4), scales=x_scales[:], in_=x_grouped[:])
 
+        st = {}
+
+        def b2_columns():
+            b2T = psum.tile([P, P], BF16, name="b2T", tag="bank")
+            nc.tensor.transpose(b2T[:], b2rows[:], identb[:])
+            nc.scalar.copy(out=b2col[:], in_=b2T[:, 0:64])
+
+        def b2_spread(k):
+            bb = psum.tile([P, 8, P], BF16, name="bb", tag="bank")
+            for r in range(8):
+                nc.tensor.transpose(
+                    bb[:, r, :], b2col[:, 8 * k + r : 8 * k + r + 1].to_broadcast([P, P]), identb[:]
+                )
+            st[("bb", k)] = bb
+
+        def b2_evac(k):
+            nc.scalar.copy(
+                out=b2t[:, 1024 * k : 1024 * (k + 1)], in_=st[("bb", k)][:].rearrange("p r c -> p (r c)")
+            )
+
         h_codes = []
         h_scales = []
         for s in range(S):
@@ -135,7 +159,6 @@ def tile_simplefusionmodule_pa_kernel(tc, x1, x2, W1, b1, W2, b2, out):
             h_codes.append(h_codes_t)
             h_scales.append(h_scales_t)
 
-        st = {}
         items = []
         for s in range(S):
             for g in range(2):
@@ -169,6 +192,9 @@ def tile_simplefusionmodule_pa_kernel(tc, x1, x2, W1, b1, W2, b2, out):
                 src = w1raw[s][:, :, G * 512 : (G + 1) * 512].rearrange("p j (m t) -> p t m j", t=4)
                 nc.scalar.copy(out=dst[:, :, 0:MS, :], in_=src[:, :, 0:MS, :])
                 nc.vector.tensor_copy(out=dst[:, :, MS:P, :], in_=src[:, :, MS:P, :])
+                b2_evac(2 * i + G)
+                if 2 * i + G + 2 < 8:
+                    b2_spread(2 * i + G + 2)
             st[("g", i)] = grouped
 
         def a_mm(i):
@@ -265,6 +291,9 @@ def tile_simplefusionmodule_pa_kernel(tc, x1, x2, W1, b1, W2, b2, out):
                 )
             nc.sync.dma_start(out=out[:, s, c0 : c0 + w], in_=o_sb[:, 0:w])
 
+        b2_columns()
+        b2_spread(0)
+        b2_spread(1)
         n = NA + len(items)
         for i in range(n + 4):
             if i < NA:

@@ -23,6 +23,7 @@ S_SHARE_32 = [15, 21]
 S_SHARE_32_LAST = [19, 23]
 MS = 32
 FAST = True
+RUN = 2
 MANUAL = True
 W2_BUFS = 5
 EVAC_ON_VECTOR = False
@@ -33,8 +34,8 @@ PIECES = [[1024, 1024], [1024, 1024], [1024, 1024], [1024, 512, 256, 256]]
 def interleave(copy, dst, src):
     if FAST:
         copy(
-            out=dst.rearrange("p (c i j) -> p c j i", i=4, j=PACK),
-            in_=src.rearrange("p j (c i) -> p c j i", i=4),
+            out=dst.rearrange("p (c i j) -> p c j i", i=RUN, j=PACK),
+            in_=src.rearrange("p j (c i) -> p c j i", i=RUN),
         )
     else:
         copy(

@@ -19,8 +19,8 @@ MAX = mybir.AluOpType.max
 P = 128
 PACK = 4
 BANK_DT = BF16
-S_SHARE_32 = [15, 21]
-S_SHARE_32_LAST = [19, 23]
+S_SHARE_32 = [16, 22]
+S_SHARE_32_LAST = [20, 24]
 MS = 32
 FAST = True
 RUN = 2

@@ -21,13 +21,15 @@ PACK = 4
 BANK_DT = BF16
 S_SHARE_32 = [16, 22]
 S_SHARE_32_LAST = [20, 24]
-MS = 32
+MS = 40
 FAST = True
 RUN = 2
 MANUAL = True
 W2_BUFS = 5
 EVAC_ON_VECTOR = False
 SUB = 1024
+NB = 4
+B2_BEFORE = [5, 6]
 PIECES = [[1024, 1024], [1024, 1024], [1024, 1024], [1024, 512, 256, 256]]
 
 
@@ -94,6 +96,9 @@ def tile_simplefusionmodule_pa_kernel(tc, x1, x2, W1, b1, W2, b2, out):
 
         def load_chunk(q):
             s, g = chunks[q]
+            if q in B2_BEFORE:
+                sb = NB // 2 + B2_BEFORE.index(q)
+                nc.sync.dma_start(out=b2t[:, sb * F2 : (sb + 1) * F2], in_=b2[sb].partition_broadcast(P))
             raw = w2raw_pool.tile([P, PACK, F2], BF16, name="w2raw_t", tag="w2raw")
             view = W2[s, 512 * g : 512 * (g + 1), :].rearrange("(p j) n -> p j n", j=PACK)
             if q == len(chunks) - 1:
@@ -193,8 +198,9 @@ def tile_simplefusionmodule_pa_kernel(tc, x1, x2, W1, b1, W2, b2, out):
                 src = w1raw[s][:, :, G * 512 : (G + 1) * 512].rearrange("p j (m t) -> p t m j", t=4)
                 nc.scalar.copy(out=dst[:, :, 0:MS, :], in_=src[:, :, 0:MS, :])
                 nc.vector.tensor_copy(out=dst[:, :, MS:P, :], in_=src[:, :, MS:P, :])
-                b2_evac(2 * i + G)
-                if 2 * i + G + 2 < 8:
+                if 2 * i + G < NB:
+                    b2_evac(2 * i + G)
+                if 2 * i + G + 2 < NB:
                     b2_spread(2 * i + G + 2)
             st[("g", i)] = grouped
 

@@ -159,9 +159,9 @@ def tile_simplefusionmodule_pa_kernel(tc, x1, x2, W1, b1, W2, b2, out):
 
         h_codes = []
         h_scales = []
-        for s in range(S):
-            h_codes_t = const.tile([P, 2 * P], U32, name="h_codes%d" % s, align_bytes=64)
-            h_scales_t = const.tile([P, 2 * P], U8, name="h_scales%d" % s, align_bytes=64)
+        for s in range(S // 2):
+            h_codes_t = const.tile([P, 4 * P], U32, name="h_codes%d" % s, align_bytes=64)
+            h_scales_t = const.tile([P, 4 * P], U8, name="h_scales%d" % s, align_bytes=64)
             h_codes.append(h_codes_t)
             h_scales.append(h_scales_t)
 
@@ -191,6 +191,18 @@ def tile_simplefusionmodule_pa_kernel(tc, x1, x2, W1, b1, W2, b2, out):
         def a_copy(i):
             s = i
             grouped = grp_pool.tile([P, PACK * SUB], BF16, name="grouped", tag="grouped", align_bytes=64)
+            if i > 0:
+                dst = grouped[:].rearrange("p (t m j) -> p t m j", t=4, j=PACK)
+                src = w1raw[s][:].rearrange("p j (m t) -> p t m j", t=4)
+                nc.scalar.copy(out=dst[:, :, 0 : 2 * MS, :], in_=src[:, :, 0 : 2 * MS, :])
+                nc.vector.tensor_copy(out=dst[:, :, 2 * MS : 2 * P, :], in_=src[:, :, 2 * MS : 2 * P, :])
+                for k in (2 * i, 2 * i + 1):
+                    if k < NB:
+                        b2_evac(k)
+                    if k + 2 < NB:
+                        b2_spread(k + 2)
+                st[("g", i)] = grouped
+                return
             for G in range(2):
                 if i == 0 and G == 1:
                     x_prepare()
@@ -211,7 +223,8 @@ def tile_simplefusionmodule_pa_kernel(tc, x1, x2, W1, b1, W2, b2, out):
             for G in range(2):
                 hp = psum.tile([P, 4, P], BANK_DT, name="hp", tag="bank")
                 for t in range(4):
-                    cols = slice(G * 512 + t * P, G * 512 + (t + 1) * P)
+                    c0 = G * 512 + t * P if i == 0 else t * 256 + G * P
+                    cols = slice(c0, c0 + P)
                     nc.tensor.matmul_mx(
                         out=hp[:, t, :],
                         lhsT=codes[:, cols].bitcast(FP8X4),
@@ -226,7 +239,10 @@ def tile_simplefusionmodule_pa_kernel(tc, x1, x2, W1, b1, W2, b2, out):
 
         def a_evac(i):
             s = i
-            hT = h_pool.tile([P, 2, 4, P], BF16, name="hT", tag="hT")
+            if s % 2 == 0:
+                hT2 = h_pool.tile([P, 2, 2, 4, P], BF16, name="hT2", tag="hT")
+                st[("hT", s // 2)] = hT2
+            hT = st[("hT", s // 2)][:, s % 2]
             for G in range(2):
                 hp = st[("hp", i)][G]
                 for t in range(4):
@@ -237,19 +253,17 @@ def tile_simplefusionmodule_pa_kernel(tc, x1, x2, W1, b1, W2, b2, out):
                         )
                     else:
                         nc.scalar.activation(out=hT[:, G, t, :], in_=hp[:, t, :], func=RELU, bias=bias)
-            st[("hT", i)] = hT
 
         def a_inter(i):
-            hg = h_pool.tile([P, 2 * P * PACK], BF16, name="hg", tag="hg", align_bytes=64)
+            hg = h_pool.tile([P, 4 * P * PACK], BF16, name="hg", tag="hg", align_bytes=64)
             nc.vector.tensor_copy(
-                out=hg[:].rearrange("p (g b t) -> p g b t", g=2, t=PACK),
-                in_=st[("hT", i)][:].rearrange("p g t b -> p g b t"),
+                out=hg[:].rearrange("p (g b t) -> p g b t", g=4, t=PACK),
+                in_=st[("hT", i)][:].rearrange("p s g t b -> p (s g) b t"),
             )
             st[("hg", i)] = hg
 
         def a_hquant(i):
-            s = i
-            nc.vector.quantize_mx(out=h_codes[s][:].bitcast(FP8X4), scales=h_scales[s][:], in_=st[("hg", i)][:])
+            nc.vector.quantize_mx(out=h_codes[i][:].bitcast(FP8X4), scales=h_scales[i][:], in_=st[("hg", i)][:])
 
         def b_copy(i):
             s, c0, w, g = items[i - NA]
@@ -274,8 +288,8 @@ def tile_simplefusionmodule_pa_kernel(tc, x1, x2, W1, b1, W2, b2, out):
                 acc = st[("acc", s, c0, nt)]
                 nc.tensor.matmul_mx(
                     out=acc[:, 0:nw],
-                    lhsT=h_codes[s][:, g * P : (g + 1) * P].bitcast(FP8X4),
-                    lhsT_scale=h_scales[s][:, g * P : (g + 1) * P],
+                    lhsT=h_codes[s // 2][:, (2 * (s % 2) + g) * P : (2 * (s % 2) + g + 1) * P].bitcast(FP8X4),
+                    lhsT_scale=h_scales[s // 2][:, (2 * (s % 2) + g) * P : (2 * (s % 2) + g + 1) * P],
                     rhs=codes[:, nt * nw : (nt + 1) * nw].bitcast(FP8X4),
                     rhs_scale=scales[:, nt * nw : (nt + 1) * nw],
                     start=(g == 0),
@@ -309,6 +323,9 @@ def tile_simplefusionmodule_pa_kernel(tc, x1, x2, W1, b1, W2, b2, out):
                 b_copy(i)
             if i == 1:
                 x_quant()
+            k = i - 4
+            if 0 <= k < NA and k % 2 == 1:
+                a_hquant(k // 2)
             k = i - 1
             if 0 <= k < n:
                 quant(k)
@@ -322,8 +339,5 @@ def tile_simplefusionmodule_pa_kernel(tc, x1, x2, W1, b1, W2, b2, out):
             elif NA <= k < n:
                 b_post(k)
             k = i - 3
-            if 0 <= k < NA:
-                a_inter(k)
-            k = i - 4
-            if 0 <= k < NA:
-                a_hquant(k)
+            if 0 <= k < NA and k % 2 == 1:
+                a_inter(k // 2)

@@ -19,8 +19,9 @@ MAX = mybir.AluOpType.max
 P = 128
 PACK = 4
 BANK_DT = BF16
-S_SHARE_32 = [16, 22]
-S_SHARE_32_LAST = [20, 24]
+S_SHARE_32 = [17, 23]
+S_SHARE_32_LAST = [21, 25]
+PT = 256
 MS = 40
 FAST = True
 RUN = 2
@@ -271,11 +272,30 @@ def tile_simplefusionmodule_pa_kernel(tc, x1, x2, W1, b1, W2, b2, out):
             sc = w * (S_SHARE_32_LAST if s == S - 1 else S_SHARE_32)[g] // 32
             grouped = grp_pool.tile([P, PACK * SUB], BF16, name="grouped", tag="grouped", align_bytes=64)
             src = w2raw[q][:, :, c0 : c0 + w]
-            interleave(nc.scalar.copy, grouped[:, 0 : PACK * sc], src[:, :, 0:sc])
+            if c0 == 0:
+                nc.scalar.copy(out=grouped[:, 0 : PACK * PT], in_=st[("pt", i)][:])
+                interleave(nc.scalar.copy, grouped[:, PACK * PT : PACK * sc], src[:, :, PT:sc])
+            else:
+                interleave(nc.scalar.copy, grouped[:, 0 : PACK * sc], src[:, :, 0:sc])
             interleave(nc.vector.tensor_copy, grouped[:, PACK * sc : PACK * w], src[:, :, sc:w])
             st[("g", i)] = grouped
             if c0 + w == F2 and q + W2_BUFS < len(chunks):
                 load_chunk(q + W2_BUFS)
+
+        def p_mm(i):
+            s, c0, w, g = items[i - NA]
+            if c0 != 0:
+                return
+            pt = psum.tile([P, PACK * PT], BF16, name="pt", tag="bank")
+            for h in range(PACK * PT // 512):
+                nc.tensor.matmul(
+                    out=pt[:, h * 512 : (h + 1) * 512].rearrange("p (n j) -> p n j", j=PACK),
+                    lhsT=identb[:],
+                    rhs=w2raw[2 * s + g][:, :, h * 128 : (h + 1) * 128].rearrange("p j n -> p n j"),
+                    start=True,
+                    stop=True,
+                )
+            st[("pt", i)] = pt
 
         def b_mm(i):
             s, c0, w, g = items[i - NA]
@@ -333,6 +353,8 @@ def tile_simplefusionmodule_pa_kernel(tc, x1, x2, W1, b1, W2, b2, out):
                     a_mm(k)
                 else:
                     b_mm(k)
+            if NA <= i + 1 < n:
+                p_mm(i + 1)
             k = i - 2
             if 0 <= k < NA:
                 a_evac(k)

@@ -19,9 +19,10 @@ MAX = mybir.AluOpType.max
 P = 128
 PACK = 4
 BANK_DT = BF16
-S_SHARE_32 = [17, 23]
-S_SHARE_32_LAST = [21, 25]
+S_SHARE_32 = [18, 23]
+S_SHARE_32_LAST = [22, 25]
 PT = 256
+PT_AT = 1024
 MS = 40
 FAST = True
 RUN = 2
@@ -272,9 +273,9 @@ def tile_simplefusionmodule_pa_kernel(tc, x1, x2, W1, b1, W2, b2, out):
             sc = w * (S_SHARE_32_LAST if s == S - 1 else S_SHARE_32)[g] // 32
             grouped = grp_pool.tile([P, PACK * SUB], BF16, name="grouped", tag="grouped", align_bytes=64)
             src = w2raw[q][:, :, c0 : c0 + w]
-            if c0 == 0:
-                nc.scalar.copy(out=grouped[:, 0 : PACK * PT], in_=st[("pt", i)][:])
+            if c0 == PT_AT:
                 interleave(nc.scalar.copy, grouped[:, PACK * PT : PACK * sc], src[:, :, PT:sc])
+                nc.scalar.copy(out=grouped[:, 0 : PACK * PT], in_=st[("pt", i)][:])
             else:
                 interleave(nc.scalar.copy, grouped[:, 0 : PACK * sc], src[:, :, 0:sc])
             interleave(nc.vector.tensor_copy, grouped[:, PACK * sc : PACK * w], src[:, :, sc:w])
@@ -284,14 +285,14 @@ def tile_simplefusionmodule_pa_kernel(tc, x1, x2, W1, b1, W2, b2, out):
 
         def p_mm(i):
             s, c0, w, g = items[i - NA]
-            if c0 != 0:
+            if c0 != PT_AT:
                 return
             pt = psum.tile([P, PACK * PT], BF16, name="pt", tag="bank")
             for h in range(PACK * PT // 512):
                 nc.tensor.matmul(
                     out=pt[:, h * 512 : (h + 1) * 512].rearrange("p (n j) -> p n j", j=PACK),
                     lhsT=identb[:],
-                    rhs=w2raw[2 * s + g][:, :, h * 128 : (h + 1) * 128].rearrange("p j n -> p n j"),
+                    rhs=w2raw[2 * s + g][:, :, c0 + h * 128 : c0 + (h + 1) * 128].rearrange("p j n -> p n j"),
                     start=True,
                     stop=True,
                 )
@@ -337,6 +338,8 @@ def tile_simplefusionmodule_pa_kernel(tc, x1, x2, W1, b1, W2, b2, out):
         b2_spread(1)
         n = NA + len(items)
         for i in range(n + 4):
+            if NA <= i + 1 < n:
+                p_mm(i + 1)
             if i < NA:
                 a_copy(i)
             elif i < n:
@@ -353,8 +356,6 @@ def tile_simplefusionmodule_pa_kernel(tc, x1, x2, W1, b1, W2, b2, out):
                     a_mm(k)
                 else:
                     b_mm(k)
-            if NA <= i + 1 < n:
-                p_mm(i + 1)
             k = i - 2
             if 0 <= k < NA:
                 a_evac(k)

@@ -19,8 +19,8 @@ MAX = mybir.AluOpType.max
 P = 128
 PACK = 4
 BANK_DT = BF16
-S_SHARE_32 = [18, 23]
-S_SHARE_32_LAST = [22, 25]
+S_SHARE_64 = [34, 45]
+S_SHARE_64_LAST = [42, 49]
 PT = 256
 PT_AT = 1024
 MS = 40
@@ -270,7 +270,7 @@ def tile_simplefusionmodule_pa_kernel(tc, x1, x2, W1, b1, W2, b2, out):
         def b_copy(i):
             s, c0, w, g = items[i - NA]
             q = 2 * s + g
-            sc = w * (S_SHARE_32_LAST if s == S - 1 else S_SHARE_32)[g] // 32
+            sc = w * (S_SHARE_64_LAST if s == S - 1 else S_SHARE_64)[g] // 64
             grouped = grp_pool.tile([P, PACK * SUB], BF16, name="grouped", tag="grouped", align_bytes=64)
             src = w2raw[q][:, :, c0 : c0 + w]
             if c0 == PT_AT:

@@ -23,15 +23,15 @@ S_SHARE_64 = [34, 45]
 S_SHARE_64_LAST = [42, 49]
 PT = 256
 PT_AT = 1024
-MS = 40
+MS = 36
 FAST = True
 RUN = 2
 MANUAL = True
 W2_BUFS = 5
 EVAC_ON_VECTOR = False
 SUB = 1024
-NB = 4
-B2_BEFORE = [5, 6]
+NB = 8
+B2_BEFORE = []
 PIECES = [[1024, 1024], [1024, 1024], [1024, 1024], [1024, 512, 256, 256]]
 
 

@@ -19,8 +19,8 @@ MAX = mybir.AluOpType.max
 P = 128
 PACK = 4
 BANK_DT = BF16
-S_SHARE_64 = [34, 45]
-S_SHARE_64_LAST = [42, 49]
+S_SHARE_64 = [[28, 43], [36, 47], [36, 47], [42, 45]]
+ALL_SCALAR_FROM = 1536
 PT = 256
 PT_AT = 1024
 MS = 36
@@ -270,7 +270,9 @@ def tile_simplefusionmodule_pa_kernel(tc, x1, x2, W1, b1, W2, b2, out):
         def b_copy(i):
             s, c0, w, g = items[i - NA]
             q = 2 * s + g
-            sc = w * (S_SHARE_64_LAST if s == S - 1 else S_SHARE_64)[g] // 64
+            sc = w * S_SHARE_64[s][g] // 64
+            if s == S - 1 and g == 1 and c0 >= ALL_SCALAR_FROM:
+                sc = w
             grouped = grp_pool.tile([P, PACK * SUB], BF16, name="grouped", tag="grouped", align_bytes=64)
             src = w2raw[q][:, :, c0 : c0 + w]
             if c0 == PT_AT:
@@ -278,7 +280,8 @@ def tile_simplefusionmodule_pa_kernel(tc, x1, x2, W1, b1, W2, b2, out):
                 nc.scalar.copy(out=grouped[:, 0 : PACK * PT], in_=st[("pt", i)][:])
             else:
                 interleave(nc.scalar.copy, grouped[:, 0 : PACK * sc], src[:, :, 0:sc])
-            interleave(nc.vector.tensor_copy, grouped[:, PACK * sc : PACK * w], src[:, :, sc:w])
+            if sc < w:
+                interleave(nc.vector.tensor_copy, grouped[:, PACK * sc : PACK * w], src[:, :, sc:w])
             st[("g", i)] = grouped
             if c0 + w == F2 and q + W2_BUFS < len(chunks):
                 load_chunk(q + W2_BUFS)

@@ -26,6 +26,7 @@ PT_AT = 1024
 MS = 36
 FAST = True
 RUN = 2
+RUN_SCALAR = 8
 MANUAL = True
 W2_BUFS = 5
 EVAC_ON_VECTOR = False
@@ -35,11 +36,11 @@ B2_BEFORE = []
 PIECES = [[1024, 1024], [1024, 1024], [1024, 1024], [1024, 512, 256, 256]]
 
 
-def interleave(copy, dst, src):
+def interleave(copy, dst, src, run=RUN):
     if FAST:
         copy(
-            out=dst.rearrange("p (c i j) -> p c j i", i=RUN, j=PACK),
-            in_=src.rearrange("p j (c i) -> p c j i", i=RUN),
+            out=dst.rearrange("p (c i j) -> p c j i", i=run, j=PACK),
+            in_=src.rearrange("p j (c i) -> p c j i", i=run),
         )
     else:
         copy(
@@ -276,10 +277,10 @@ def tile_simplefusionmodule_pa_kernel(tc, x1, x2, W1, b1, W2, b2, out):
             grouped = grp_pool.tile([P, PACK * SUB], BF16, name="grouped", tag="grouped", align_bytes=64)
             src = w2raw[q][:, :, c0 : c0 + w]
             if c0 == PT_AT:
-                interleave(nc.scalar.copy, grouped[:, PACK * PT : PACK * sc], src[:, :, PT:sc])
+                interleave(nc.scalar.copy, grouped[:, PACK * PT : PACK * sc], src[:, :, PT:sc], RUN_SCALAR)
                 nc.scalar.copy(out=grouped[:, 0 : PACK * PT], in_=st[("pt", i)][:])
             else:
-                interleave(nc.scalar.copy, grouped[:, 0 : PACK * sc], src[:, :, 0:sc])
+                interleave(nc.scalar.copy, grouped[:, 0 : PACK * sc], src[:, :, 0:sc], RUN_SCALAR)
             if sc < w:
                 interleave(nc.vector.tensor_copy, grouped[:, PACK * sc : PACK * w], src[:, :, sc:w])
             st[("g", i)] = grouped

@@ -27,6 +27,7 @@ MS = 36
 FAST = True
 RUN = 2
 RUN_SCALAR = 8
+LEAD_LAST = 3
 MANUAL = True
 W2_BUFS = 5
 EVAC_ON_VECTOR = False
@@ -341,9 +342,12 @@ def tile_simplefusionmodule_pa_kernel(tc, x1, x2, W1, b1, W2, b2, out):
         b2_spread(0)
         b2_spread(1)
         n = NA + len(items)
+        ahead = set()
         for i in range(n + 4):
-            if NA <= i + 1 < n:
-                p_mm(i + 1)
+            for j in range(i + 1, i + 1 + LEAD_LAST):
+                if NA <= j < n and j not in ahead and (j == i + 1 or items[j - NA][0::3] == (S - 1, 1)):
+                    ahead.add(j)
+                    p_mm(j)
             if i < NA:
                 a_copy(i)
             elif i < n:

@@ -15,6 +15,7 @@ FP8X4 = mybir.dt.float8_e4m3fn_x4
 RELU = mybir.ActivationFunctionType.Relu
 ADD = mybir.AluOpType.add
 MAX = mybir.AluOpType.max
+MULT = mybir.AluOpType.mult
 
 P = 128
 PACK = 4
@@ -28,6 +29,8 @@ FAST = True
 RUN = 2
 RUN_SCALAR = 8
 LEAD_LAST = 3
+GC = 128
+G_FROM_SCALAR = 96
 MANUAL = True
 W2_BUFS = 5
 EVAC_ON_VECTOR = False
@@ -269,12 +272,35 @@ def tile_simplefusionmodule_pa_kernel(tc, x1, x2, W1, b1, W2, b2, out):
         def a_hquant(i):
             nc.vector.quantize_mx(out=h_codes[i][:].bitcast(FP8X4), scales=h_scales[i][:], in_=st[("hg", i)][:])
 
+        def g_width(i):
+            s, c0, w, g = items[i - NA]
+            return GC if s > 0 and g == 0 and c0 <= 1024 else 0
+
+        def g_copy(i):
+            s, c0, w, g = items[i - NA]
+            q = 2 * s + g
+            grouped = st[("g", i)]
+            nc.vector.memset(grouped[:, PACK * (w - GC) : PACK * (w - GC) + 2], 0.0)
+            nc.gpsimd.tensor_scalar(
+                out=grouped[:, PACK * (w - GC) : PACK * w].rearrange("p (c j) -> p c j", j=PACK),
+                in0=w2raw[q][:, :, c0 + w - GC : c0 + w].rearrange("p j c -> p c j"),
+                scalar1=1.0,
+                scalar2=0.0,
+                op0=MULT,
+                op1=ADD,
+            )
+            if c0 + w == F2 and q + W2_BUFS < len(chunks):
+                load_chunk(q + W2_BUFS)
+
         def b_copy(i):
             s, c0, w, g = items[i - NA]
             q = 2 * s + g
             sc = w * S_SHARE_64[s][g] // 64
             if s == S - 1 and g == 1 and c0 >= ALL_SCALAR_FROM:
                 sc = w
+            gw = g_width(i)
+            if gw > 0 and w == SUB:
+                sc -= G_FROM_SCALAR
             grouped = grp_pool.tile([P, PACK * SUB], BF16, name="grouped", tag="grouped", align_bytes=64)
             src = w2raw[q][:, :, c0 : c0 + w]
             if c0 == PT_AT:
@@ -282,10 +308,12 @@ def tile_simplefusionmodule_pa_kernel(tc, x1, x2, W1, b1, W2, b2, out):
                 nc.scalar.copy(out=grouped[:, 0 : PACK * PT], in_=st[("pt", i)][:])
             else:
                 interleave(nc.scalar.copy, grouped[:, 0 : PACK * sc], src[:, :, 0:sc], RUN_SCALAR)
-            if sc < w:
-                interleave(nc.vector.tensor_copy, grouped[:, PACK * sc : PACK * w], src[:, :, sc:w])
+            if sc < w - gw:
+                interleave(nc.vector.tensor_copy, grouped[:, PACK * sc : PACK * (w - gw)], src[:, :, sc : w - gw])
             st[("g", i)] = grouped
-            if c0 + w == F2 and q + W2_BUFS < len(chunks):
+            if gw > 0:
+                g_copy(i)
+            elif c0 + w == F2 and q + W2_BUFS < len(chunks):
                 load_chunk(q + W2_BUFS)
 
         def p_mm(i):

@@ -29,6 +29,8 @@ FAST = True
 RUN = 2
 RUN_SCALAR = 8
 LEAD_LAST = 3
+LEAD = 3
+GRP_BUFS = 8
 GC = 128
 G_FROM_SCALAR = 96
 MANUAL = True
@@ -57,9 +59,8 @@ def tile_simplefusionmodule_pa_kernel(tc, x1, x2, W1, b1, W2, b2, out):
     nc = tc.nc
     with ExitStack() as ctx:
         const = ctx.enter_context(tc.tile_pool(name="const", bufs=1))
-        w1raw_pool = ctx.enter_context(tc.tile_pool(name="w1raw", bufs=S))
         w2raw_pool = ctx.enter_context(tc.tile_pool(name="w2raw", bufs=W2_BUFS))
-        grp_pool = ctx.enter_context(tc.tile_pool(name="grp", bufs=4))
+        grp_pool = ctx.enter_context(tc.tile_pool(name="grp", bufs=GRP_BUFS))
         code_pool = ctx.enter_context(tc.tile_pool(name="code", bufs=3))
         h_pool = ctx.enter_context(tc.tile_pool(name="hpool", bufs=2))
         o_pool = ctx.enter_context(tc.tile_pool(name="opool", bufs=4))
@@ -80,9 +81,10 @@ def tile_simplefusionmodule_pa_kernel(tc, x1, x2, W1, b1, W2, b2, out):
         nc.vector.memset(b2rows[64:128, :], 0.0)
 
         w1raw = []
-        for s in range(S):
-            w1raw_t = w1raw_pool.tile([P, PACK, F1], BF16, name="w1raw_t", tag="w1raw")
-            w1raw.append(w1raw_t)
+        for s in range(S // 2):
+            w1raw_t = w2raw_pool.tile([P, 2, PACK, F1], BF16, name="w1raw_t", tag="w2raw")
+            w1raw.append(w1raw_t[:, 0])
+            w1raw.append(w1raw_t[:, 1])
         w1view = [W1[s].rearrange("(p j) c -> p j c", j=PACK) for s in range(S)]
         x_sb = const.tile([P, S, K1], BF16, name="x_sb")
         b1col = const.tile([P, 2 * S, PACK], BF16, name="b1col")
@@ -94,7 +96,7 @@ def tile_simplefusionmodule_pa_kernel(tc, x1, x2, W1, b1, W2, b2, out):
         nc.sync.dma_start(out=x_sb[:, :, D:K1], in_=x2)
         nc.sync.dma_start(out=w1raw[0][:, :, 512:1024], in_=w1view[0][:, :, 512:1024])
         for s in range(1, S):
-            nc.sync.dma_start(out=w1raw[s][:], in_=w1view[s])
+            nc.sync.dma_start(out=w1raw[s], in_=w1view[s])
             if s == 1:
                 nc.sync.dma_start(out=b1col[:], in_=b1.rearrange("s (g p t) -> p (s g) t", g=2, t=PACK))
 
@@ -200,7 +202,7 @@ def tile_simplefusionmodule_pa_kernel(tc, x1, x2, W1, b1, W2, b2, out):
             grouped = grp_pool.tile([P, PACK * SUB], BF16, name="grouped", tag="grouped", align_bytes=64)
             if i > 0:
                 dst = grouped[:].rearrange("p (t m j) -> p t m j", t=4, j=PACK)
-                src = w1raw[s][:].rearrange("p j (m t) -> p t m j", t=4)
+                src = w1raw[s].rearrange("p j (m t) -> p t m j", t=4)
                 nc.scalar.copy(out=dst[:, :, 0 : 2 * MS, :], in_=src[:, :, 0 : 2 * MS, :])
                 nc.vector.tensor_copy(out=dst[:, :, 2 * MS : 2 * P, :], in_=src[:, :, 2 * MS : 2 * P, :])
                 for k in (2 * i, 2 * i + 1):
@@ -366,14 +368,19 @@ def tile_simplefusionmodule_pa_kernel(tc, x1, x2, W1, b1, W2, b2, out):
                 )
             nc.sync.dma_start(out=out[:, s, c0 : c0 + w], in_=o_sb[:, 0:w])
 
+        def pe_lead(j):
+            if items[j - NA][0::3] == (S - 1, 1):
+                return LEAD_LAST
+            return 1 if j < NA + 5 else 2
+
         b2_columns()
         b2_spread(0)
         b2_spread(1)
         n = NA + len(items)
         ahead = set()
         for i in range(n + 4):
-            for j in range(i + 1, i + 1 + LEAD_LAST):
-                if NA <= j < n and j not in ahead and (j == i + 1 or items[j - NA][0::3] == (S - 1, 1)):
+            for j in range(i + 1, i + 1 + LEAD):
+                if NA <= j < n and j not in ahead and j - i <= pe_lead(j):
                     ahead.add(j)
                     p_mm(j)
             if i < NA:

@@ -20,11 +20,11 @@ MULT = mybir.AluOpType.mult
 P = 128
 PACK = 4
 BANK_DT = BF16
-S_SHARE_64 = [[28, 43], [36, 47], [36, 47], [42, 45]]
+S_SHARE_128 = [[58, 89], [74, 97], [74, 97], [86, 92]]
 ALL_SCALAR_FROM = 1536
 PT = 256
 PT_AT = 1024
-MS = 36
+MS = 38
 FAST = True
 RUN = 2
 RUN_SCALAR = 8
@@ -297,7 +297,7 @@ def tile_simplefusionmodule_pa_kernel(tc, x1, x2, W1, b1, W2, b2, out):
         def b_copy(i):
             s, c0, w, g = items[i - NA]
             q = 2 * s + g
-            sc = w * S_SHARE_64[s][g] // 64
+            sc = w * S_SHARE_128[s][g] // 128 // 8 * 8
             if s == S - 1 and g == 1 and c0 >= ALL_SCALAR_FROM:
                 sc = w
             gw = g_width(i)

from contextlib import ExitStack

import concourse.mybir as mybir
from concourse.masks import make_identity

B, S, D, F1, F2 = 128, 4, 256, 1024, 2048
K1 = 2 * D
FLOPS = 2 * B * S * (K1 * F1 + F1 * F2)

F32 = mybir.dt.float32
BF16 = mybir.dt.bfloat16
U32 = mybir.dt.uint32
U8 = mybir.dt.uint8
FP8X4 = mybir.dt.float8_e4m3fn_x4
RELU = mybir.ActivationFunctionType.Relu
ADD = mybir.AluOpType.add
MAX = mybir.AluOpType.max
MULT = mybir.AluOpType.mult

P = 128
PACK = 4
BANK_DT = BF16
S_SHARE_128 = [[58, 89], [74, 97], [74, 97], [86, 92]]
ALL_SCALAR_FROM = 1536
PT = 256
PT_AT = 1024
MS = 38
FAST = True
RUN = 2
RUN_SCALAR = 8
LEAD_LAST = 3
LEAD = 3
GRP_BUFS = 8
GC = 128
G_FROM_SCALAR = 96
MANUAL = True
W2_BUFS = 5
EVAC_ON_VECTOR = False
SUB = 1024
NB = 8
B2_BEFORE = []
PIECES = [[1024, 1024], [1024, 1024], [1024, 1024], [1024, 512, 256, 256]]


def interleave(copy, dst, src, run=RUN):
    if FAST:
        copy(
            out=dst.rearrange("p (c i j) -> p c j i", i=run, j=PACK),
            in_=src.rearrange("p j (c i) -> p c j i", i=run),
        )
    else:
        copy(
            out=dst.rearrange("p (w j) -> p w j", j=PACK),
            in_=src.rearrange("p j w -> p w j"),
        )


def tile_simplefusionmodule_pa_kernel(tc, x1, x2, W1, b1, W2, b2, out):
    nc = tc.nc
    with ExitStack() as ctx:
        const = ctx.enter_context(tc.tile_pool(name="const", bufs=1))
        w2raw_pool = ctx.enter_context(tc.tile_pool(name="w2raw", bufs=W2_BUFS))
        grp_pool = ctx.enter_context(tc.tile_pool(name="grp", bufs=GRP_BUFS))
        code_pool = ctx.enter_context(tc.tile_pool(name="code", bufs=3))
        h_pool = ctx.enter_context(tc.tile_pool(name="hpool", bufs=2))
        o_pool = ctx.enter_context(tc.tile_pool(name="opool", bufs=4))
        psum = ctx.enter_context(tc.psum_pool(name="psum", bufs=8))
        if MANUAL:
            ctx.enter_context(tc.manual_schedule())

        warm_in = const.tile([P, 1], F32, name="warm_in")
        warm_out = const.tile([P, 1], F32, name="warm_out")
        nc.vector.memset(warm_in[:], 0.0)
        nc.scalar.activation(out=warm_out[:], in_=warm_in[:], func=RELU)
        ident = const.tile([P, P], F32, name="ident")
        make_identity(nc, ident[:])
        identb = const.tile([P, P], BF16, name="identb")
        make_identity(nc, identb[:])
        b2rows = const.tile([P, P], BF16, name="b2rows")
        b2col = const.tile([P, 64], BF16, name="b2col")
        nc.vector.memset(b2rows[64:128, :], 0.0)

        w1raw = []
        for s in range(S // 2):
            w1raw_t = w2raw_pool.tile([P, 2, PACK, F1], BF16, name="w1raw_t", tag="w2raw")
            w1raw.append(w1raw_t[:, 0])
            w1raw.append(w1raw_t[:, 1])
        w1view = [W1[s].rearrange("(p j) c -> p j c", j=PACK) for s in range(S)]
        x_sb = const.tile([P, S, K1], BF16, name="x_sb")
        b1col = const.tile([P, 2 * S, PACK], BF16, name="b1col")
        b2t = const.tile([P, S * F2], BF16, name="b2t")

        nc.sync.dma_start(out=b2rows[0:64, :], in_=b2.rearrange("s (j c) -> (s j) c", c=P))
        nc.sync.dma_start(out=w1raw[0][:, :, 0:512], in_=w1view[0][:, :, 0:512])
        nc.sync.dma_start(out=x_sb[:, :, 0:D], in_=x1)
        nc.sync.dma_start(out=x_sb[:, :, D:K1], in_=x2)
        nc.sync.dma_start(out=w1raw[0][:, :, 512:1024], in_=w1view[0][:, :, 512:1024])
        for s in range(1, S):
            nc.sync.dma_start(out=w1raw[s], in_=w1view[s])
            if s == 1:
                nc.sync.dma_start(out=b1col[:], in_=b1.rearrange("s (g p t) -> p (s g) t", g=2, t=PACK))

        chunks = [(s, g) for s in range(S) for g in range(2)]
        w2raw = {}

        def load_chunk(q):
            s, g = chunks[q]
            if q in B2_BEFORE:
                sb = NB // 2 + B2_BEFORE.index(q)
                nc.sync.dma_start(out=b2t[:, sb * F2 : (sb + 1) * F2], in_=b2[sb].partition_broadcast(P))
            raw = w2raw_pool.tile([P, PACK, F2], BF16, name="w2raw_t", tag="w2raw")
            view = W2[s, 512 * g : 512 * (g + 1), :].rearrange("(p j) n -> p j n", j=PACK)
            if q == len(chunks) - 1:
                c0 = 0
                for w in PIECES[s]:
                    nc.sync.dma_start(out=raw[:, :, c0 : c0 + w], in_=view[:, :, c0 : c0 + w])
                    c0 += w
            else:
                nc.sync.dma_start(out=raw[:], in_=view)
            w2raw[q] = raw

        for q in range(W2_BUFS):
            load_chunk(q)

        x_words = x_sb[:].rearrange("p s k -> p (s k)").bitcast(F32)
        x_grouped = const.tile([P, S * P * PACK], BF16, name="x_grouped", align_bytes=64)
        x_codes = const.tile([P, S * P], U32, name="x_codes", align_bytes=64)
        x_scales = const.tile([P, S * P], U8, name="x_scales", align_bytes=64)

        def x_prepare():
            for half in range(2):
                xt = psum.tile([P, 2, 2, P], F32, name="xt", tag="bank")
                for s2 in range(2):
                    s = 2 * half + s2
                    for u in range(2):
                        nc.tensor.transpose(
                            xt[:, s2, u, :], x_words[:, 256 * s + u : 256 * (s + 1) : 2], ident[:]
                        )
                nc.scalar.copy(
                    out=x_grouped[:, half * 1024 : (half + 1) * 1024]
                    .bitcast(F32)
                    .rearrange("p (s b u) -> p s b u", s=2, u=2),
                    in_=xt[:].rearrange("p s u b -> p s b u"),
                )

        def x_quant():
            nc.vector.quantize_mx(out=x_codes[:].bitcast(FP8X4), scales=x_scales[:], in_=x_grouped[:])

        st = {}

        def b2_columns():
            b2T = psum.tile([P, P], BF16, name="b2T", tag="bank")
            nc.tensor.transpose(b2T[:], b2rows[:], identb[:])
            nc.scalar.copy(out=b2col[:], in_=b2T[:, 0:64])

        def b2_spread(k):
            bb = psum.tile([P, 8, P], BF16, name="bb", tag="bank")
            for r in range(8):
                nc.tensor.transpose(
                    bb[:, r, :], b2col[:, 8 * k + r : 8 * k + r + 1].to_broadcast([P, P]), identb[:]
                )
            st[("bb", k)] = bb

        def b2_evac(k):
            nc.scalar.copy(
                out=b2t[:, 1024 * k : 1024 * (k + 1)], in_=st[("bb", k)][:].rearrange("p r c -> p (r c)")
            )

        h_codes = []
        h_scales = []
        for s in range(S // 2):
            h_codes_t = const.tile([P, 4 * P], U32, name="h_codes%d" % s, align_bytes=64)
            h_scales_t = const.tile([P, 4 * P], U8, name="h_scales%d" % s, align_bytes=64)
            h_codes.append(h_codes_t)
            h_scales.append(h_scales_t)

        items = []
        for s in range(S):
            for g in range(2):
                c0 = 0
                for w in PIECES[s]:
                    items.append((s, c0, w, g))
                    c0 += w
        NA = S

        def width_of(i):
            if i < NA:
                return SUB
            return items[i - NA][2]

        def quant(i):
            w = width_of(i)
            codes = code_pool.tile([P, SUB], U32, name="codes", tag="codes", align_bytes=64)
            scales = code_pool.tile([P, SUB], U8, name="scales", tag="scales", align_bytes=64)
            nc.vector.quantize_mx(
                out=codes[:, 0:w].bitcast(FP8X4), scales=scales[:, 0:w], in_=st[("g", i)][:, 0 : PACK * w]
            )
            st[("c", i)] = (codes, scales)

        def a_copy(i):
            s = i
            grouped = grp_pool.tile([P, PACK * SUB], BF16, name="grouped", tag="grouped", align_bytes=64)
            if i > 0:
                dst = grouped[:].rearrange("p (t m j) -> p t m j", t=4, j=PACK)
                src = w1raw[s].rearrange("p j (m t) -> p t m j", t=4)
                nc.scalar.copy(out=dst[:, :, 0 : 2 * MS, :], in_=src[:, :, 0 : 2 * MS, :])
                nc.vector.tensor_copy(out=dst[:, :, 2 * MS : 2 * P, :], in_=src[:, :, 2 * MS : 2 * P, :])
                for k in (2 * i, 2 * i + 1):
                    if k < NB:
                        b2_evac(k)
                    if k + 2 < NB:
                        b2_spread(k + 2)
                st[("g", i)] = grouped
                return
            for G in range(2):
                if i == 0 and G == 1:
                    x_prepare()
                dst = grouped[:, G * 2048 : (G + 1) * 2048].rearrange("p (t m j) -> p t m j", t=4, j=PACK)
                src = w1raw[s][:, :, G * 512 : (G + 1) * 512].rearrange("p j (m t) -> p t m j", t=4)
                nc.scalar.copy(out=dst[:, :, 0:MS, :], in_=src[:, :, 0:MS, :])
                nc.vector.tensor_copy(out=dst[:, :, MS:P, :], in_=src[:, :, MS:P, :])
                if 2 * i + G < NB:
                    b2_evac(2 * i + G)
                if 2 * i + G + 2 < NB:
                    b2_spread(2 * i + G + 2)
            st[("g", i)] = grouped

        def a_mm(i):
            s = i
            codes, scales = st[("c", i)]
            banks = []
            for G in range(2):
                hp = psum.tile([P, 4, P], BANK_DT, name="hp", tag="bank")
                for t in range(4):
                    c0 = G * 512 + t * P if i == 0 else t * 256 + G * P
                    cols = slice(c0, c0 + P)
                    nc.tensor.matmul_mx(
                        out=hp[:, t, :],
                        lhsT=codes[:, cols].bitcast(FP8X4),
                        lhsT_scale=scales[:, cols],
                        rhs=x_codes[:, s * P : (s + 1) * P].bitcast(FP8X4),
                        rhs_scale=x_scales[:, s * P : (s + 1) * P],
                        start=True,
                        stop=True,
                    )
                banks.append(hp)
            st[("hp", i)] = banks

        def a_evac(i):
            s = i
            if s % 2 == 0:
                hT2 = h_pool.tile([P, 2, 2, 4, P], BF16, name="hT2", tag="hT")
                st[("hT", s // 2)] = hT2
            hT = st[("hT", s // 2)][:, s % 2]
            for G in range(2):
                hp = st[("hp", i)][G]
                for t in range(4):
                    bias = b1col[:, 2 * s + G, t : t + 1]
                    if EVAC_ON_VECTOR:
                        nc.vector.tensor_scalar(
                            out=hT[:, G, t, :], in0=hp[:, t, :], scalar1=bias, scalar2=0.0, op0=ADD, op1=MAX
                        )
                    else:
                        nc.scalar.activation(out=hT[:, G, t, :], in_=hp[:, t, :], func=RELU, bias=bias)

        def a_inter(i):
            hg = h_pool.tile([P, 4 * P * PACK], BF16, name="hg", tag="hg", align_bytes=64)
            nc.vector.tensor_copy(
                out=hg[:].rearrange("p (g b t) -> p g b t", g=4, t=PACK),
                in_=st[("hT", i)][:].rearrange("p s g t b -> p (s g) b t"),
            )
            st[("hg", i)] = hg

        def a_hquant(i):
            nc.vector.quantize_mx(out=h_codes[i][:].bitcast(FP8X4), scales=h_scales[i][:], in_=st[("hg", i)][:])

        def g_width(i):
            s, c0, w, g = items[i - NA]
            return GC if s > 0 and g == 0 and c0 <= 1024 else 0

        def g_copy(i):
            s, c0, w, g = items[i - NA]
            q = 2 * s + g
            grouped = st[("g", i)]
            nc.vector.memset(grouped[:, PACK * (w - GC) : PACK * (w - GC) + 2], 0.0)
            nc.gpsimd.tensor_scalar(
                out=grouped[:, PACK * (w - GC) : PACK * w].rearrange("p (c j) -> p c j", j=PACK),
                in0=w2raw[q][:, :, c0 + w - GC : c0 + w].rearrange("p j c -> p c j"),
                scalar1=1.0,
                scalar2=0.0,
                op0=MULT,
                op1=ADD,
            )
            if c0 + w == F2 and q + W2_BUFS < len(chunks):
                load_chunk(q + W2_BUFS)

        def b_copy(i):
            s, c0, w, g = items[i - NA]
            q = 2 * s + g
            sc = w * S_SHARE_128[s][g] // 128 // 8 * 8
            if s == S - 1 and g == 1 and c0 >= ALL_SCALAR_FROM:
                sc = w
            gw = g_width(i)
            if gw > 0 and w == SUB:
                sc -= G_FROM_SCALAR
            grouped = grp_pool.tile([P, PACK * SUB], BF16, name="grouped", tag="grouped", align_bytes=64)
            src = w2raw[q][:, :, c0 : c0 + w]
            if c0 == PT_AT:
                interleave(nc.scalar.copy, grouped[:, PACK * PT : PACK * sc], src[:, :, PT:sc], RUN_SCALAR)
                nc.scalar.copy(out=grouped[:, 0 : PACK * PT], in_=st[("pt", i)][:])
            else:
                interleave(nc.scalar.copy, grouped[:, 0 : PACK * sc], src[:, :, 0:sc], RUN_SCALAR)
            if sc < w - gw:
                interleave(nc.vector.tensor_copy, grouped[:, PACK * sc : PACK * (w - gw)], src[:, :, sc : w - gw])
            st[("g", i)] = grouped
            if gw > 0:
                g_copy(i)
            elif c0 + w == F2 and q + W2_BUFS < len(chunks):
                load_chunk(q + W2_BUFS)

        def p_mm(i):
            s, c0, w, g = items[i - NA]
            if c0 != PT_AT:
                return
            pt = psum.tile([P, PACK * PT], BF16, name="pt", tag="bank")
            for h in range(PACK * PT // 512):
                nc.tensor.matmul(
                    out=pt[:, h * 512 : (h + 1) * 512].rearrange("p (n j) -> p n j", j=PACK),
                    lhsT=identb[:],
                    rhs=w2raw[2 * s + g][:, :, c0 + h * 128 : c0 + (h + 1) * 128].rearrange("p j n -> p n j"),
                    start=True,
                    stop=True,
                )
            st[("pt", i)] = pt

        def b_mm(i):
            s, c0, w, g = items[i - NA]
            codes, scales = st[("c", i)]
            nw = min(w, 512)
            for nt in range(w // nw):
                if g == 0:
                    acc = psum.tile([P, 512], F32, name="acc", tag="bank")
                    st[("acc", s, c0, nt)] = acc
                acc = st[("acc", s, c0, nt)]
                nc.tensor.matmul_mx(
                    out=acc[:, 0:nw],
                    lhsT=h_codes[s // 2][:, (2 * (s % 2) + g) * P : (2 * (s % 2) + g + 1) * P].bitcast(FP8X4),
                    lhsT_scale=h_scales[s // 2][:, (2 * (s % 2) + g) * P : (2 * (s % 2) + g + 1) * P],
                    rhs=codes[:, nt * nw : (nt + 1) * nw].bitcast(FP8X4),
                    rhs_scale=scales[:, nt * nw : (nt + 1) * nw],
                    start=(g == 0),
                    stop=(g == 1),
                )

        def b_post(i):
            s, c0, w, g = items[i - NA]
            if g == 0:
                return
            nw = min(w, 512)
            o_sb = o_pool.tile([P, SUB], F32, name="o_sb", tag="o_sb")
            for nt in range(w // nw):
                n0 = s * F2 + c0 + nt * nw
                nc.vector.tensor_tensor(
                    out=o_sb[:, nt * nw : (nt + 1) * nw],
                    in0=st[("acc", s, c0, nt)][:, 0:nw],
                    in1=b2t[:, n0 : n0 + nw],
                    op=ADD,
                )
            nc.sync.dma_start(out=out[:, s, c0 : c0 + w], in_=o_sb[:, 0:w])

        def pe_lead(j):
            if items[j - NA][0::3] == (S - 1, 1):
                return LEAD_LAST
            return 1 if j < NA + 5 else 2

        b2_columns()
        b2_spread(0)
        b2_spread(1)
        n = NA + len(items)
        ahead = set()
        for i in range(n + 4):
            for j in range(i + 1, i + 1 + LEAD):
                if NA <= j < n and j not in ahead and j - i <= pe_lead(j):
                    ahead.add(j)
                    p_mm(j)
            if i < NA:
                a_copy(i)
            elif i < n:
                b_copy(i)
            if i == 1:
                x_quant()
            k = i - 4
            if 0 <= k < NA and k % 2 == 1:
                a_hquant(k // 2)
            k = i - 1
            if 0 <= k < n:
                quant(k)
                if k < NA:
                    a_mm(k)
                else:
                    b_mm(k)
            k = i - 2
            if 0 <= k < NA:
                a_evac(k)
            elif NA <= k < n:
                b_post(k)
            k = i - 3
            if 0 <= k < NA and k % 2 == 1:
                a_inter(k // 2)
